import numpy as np
import ml_dtypes


def mxq(x, axis, fmt="e4m3"):
    dtype, down = {"e4m3": (ml_dtypes.float8_e4m3fn, 7), "e5m2": (ml_dtypes.float8_e5m2, 14)}[fmt]
    v = np.moveaxis(np.asarray(x, np.float32).astype(ml_dtypes.bfloat16).astype(np.float64), axis, -1)
    blocks = v.reshape(v.shape[:-1] + (-1, 32))
    amax = np.abs(blocks).max(-1, keepdims=True)
    byte = np.maximum(np.where(amax > 0, np.frexp(amax)[1] - 1 + 127, 0) - down, 1)
    scale = np.exp2(byte - 127.0)
    codes = (blocks / scale).astype(np.float32).astype(dtype).astype(np.float64)
    return np.moveaxis((codes * scale).reshape(v.shape), -1, axis)


WIDE = False


def mx_kscale(k):
    if not WIDE:
        return np.ones(k)
    levels = np.array([10, -10, 5, -5, 0])
    if k % 512:
        return np.exp2(np.random.permutation(np.resize(levels, k // 32))).repeat(32)
    a = np.empty((k // 512, 16))
    for p in range(k // 512):
        a[p, :8] = np.random.permutation(np.resize(levels, 8))
        for g in range(8):
            far = levels[np.abs(levels - a[p, g]) >= 10]
            a[p, g + 8] = far[np.random.randint(len(far))]
    return np.exp2(a.ravel()).repeat(32)


BF16 = ml_dtypes.bfloat16


def bf(x):
    return np.asarray(x, np.float32).astype(BF16)


def f64(x):
    return np.asarray(x).astype(np.float64)


B, N1, N2, D, H, DH = 4, 384, 128, 1024, 8, 128
E = H * DH


def rope_tables(n, d):
    inv = 1.0 / (10000.0 ** (np.arange(0, d, 2) / d))
    ang = np.outer(np.arange(n), inv)
    return np.repeat(np.cos(ang), 2, axis=-1), np.repeat(np.sin(ang), 2, axis=-1)


def apply_rope(x, cos, sin):
    xr = x.reshape(x.shape[:-1] + (-1, 2))
    x_real, x_imag = xr[..., 0], xr[..., 1]
    x_rot = np.stack([-x_imag, x_real], axis=-1).reshape(x.shape)
    return x * cos[None, None] + x_rot * sin[None, None]


def split_heads(t):
    b, n, _ = t.shape
    return t.reshape(b, n, H, DH).transpose(0, 2, 1, 3)


def setup_inputs():
    s1, s2 = mx_kscale(D), mx_kscale(D)
    cos1, sin1 = rope_tables(N1, DH)
    cos2, sin2 = rope_tables(N2, DH)

    def w(s):
        return bf(np.random.standard_normal((D, E)) * 1.4 / np.sqrt(D) / s[:, None])

    def b():
        return bf(np.random.standard_normal(E) * 0.3)

    return {"x_1": bf(np.random.standard_normal((B, N1, D)) * s1), "x_2": bf(np.random.standard_normal((B, N2, D)) * s2),
            "cos1": bf(cos1), "sin1": bf(sin1), "cos2": bf(cos2), "sin2": bf(sin2),
            "wq1": w(s1), "bq1": b(), "wk1": w(s1), "bk1": b(),
            "wq2": w(s2), "bq2": b(), "wk2": w(s2), "bk2": b()}


def reference(x_1, x_2, cos1, sin1, cos2, sin2, wq1, bq1, wk1, bk1, wq2, bq2, wk2, bk2):
    x1q = mxq(f64(x_1), 2, "e4m3")
    x2q = mxq(f64(x_2), 2, "e4m3")
    q = np.concatenate([(x1q @ mxq(f64(wq1), 0, "e4m3")) + f64(bq1),
                        (x2q @ mxq(f64(wq2), 0, "e4m3")) + f64(bq2)], axis=1)
    k = np.concatenate([(x1q @ mxq(f64(wk1), 0, "e4m3")) + f64(bk1),
                        (x2q @ mxq(f64(wk2), 0, "e4m3")) + f64(bk2)], axis=1)
    q, k = split_heads(q), split_heads(k)
    q = q * (DH ** -0.5)
    cos = np.concatenate([f64(cos1), f64(cos2)], axis=0)
    sin = np.concatenate([f64(sin1), f64(sin2)], axis=0)
    return apply_rope(q, cos, sin), apply_rope(k, cos, sin)

@@ -1,0 +1,252 @@
+from contextlib import ExitStack
+
+import concourse.masks as masks
+import concourse.mybir as mybir
+
+F32 = mybir.dt.float32
+BF16 = mybir.dt.bfloat16
+U32 = mybir.dt.uint32
+U8 = mybir.dt.uint8
+FP8X4 = mybir.dt.float8_e4m3fn_x4
+MULT = mybir.AluOpType.mult
+ADD = mybir.AluOpType.add
+IDENTITY = mybir.ActivationFunctionType.Identity
+
+P = 128
+D = 1024
+PASSES = 2
+WIDE = 512
+N1 = 384
+Q_SCALE = P ** -0.5
+FLOPS = 2 * 2048 * 1024 * 2048
+
+
+def tile_dualmultiheadattention_pa_kernel(
+    tc, x_1, x_2, cos1, sin1, cos2, sin2, wq1, bq1, wk1, bk1, wq2, bq2, wk2, bk2, out_0, out_1
+):
+    nc = tc.nc
+    projections = [
+        (wq1, bq1, out_0, Q_SCALE, (0, 1, 2)),
+        (wk1, bk1, out_1, 1.0, (0, 1, 2)),
+        (wq2, bq2, out_0, Q_SCALE, (3,)),
+        (wk2, bk2, out_1, 1.0, (3,)),
+    ]
+    rounds = [(sl, grp) for sl in range(8) for grp in projections[sl // 2][4]]
+    n_rounds = len(rounds)
+
+    with ExitStack() as ctx:
+        const = ctx.enter_context(tc.tile_pool(name="const", bufs=1))
+        raw = ctx.enter_context(tc.tile_pool(name="raw", bufs=1))
+        x_grouped_pool = ctx.enter_context(tc.tile_pool(name="x_grouped", bufs=2))
+        w_grouped_pool = ctx.enter_context(tc.tile_pool(name="w_grouped", bufs=2))
+        w_codes_pool = ctx.enter_context(tc.tile_pool(name="w_codes", bufs=4))
+        biased_pool = ctx.enter_context(tc.tile_pool(name="biased", bufs=8))
+        products_pool = ctx.enter_context(tc.tile_pool(name="products", bufs=3))
+        y1_pool = ctx.enter_context(tc.tile_pool(name="y1", bufs=3))
+        y2_pool = ctx.enter_context(tc.tile_pool(name="y2", bufs=3))
+        mx_banks = ctx.enter_context(tc.psum_pool(name="mx_banks", bufs=3))
+        back_banks = ctx.enter_context(tc.psum_pool(name="back_banks", bufs=5))
+        ctx.enter_context(tc.manual_schedule())
+
+        ident = const.tile([P, P], F32, name="ident")
+        masks.make_identity(nc, ident[:])
+
+        bias_rows = const.tile([P, P], BF16, name="bias_rows")
+        nc.vector.memset(bias_rows[:], 0.0)
+        for w in range(4):
+            nc.scalar.dma_start(
+                out=bias_rows[8 * w : 8 * w + 8, :], in_=projections[w][1].rearrange("(h c) -> h c", c=P)
+            )
+        cos_bf = const.tile([P, 4, P], BF16, name="cos_bf")
+        sin_bf = const.tile([P, 4, P], BF16, name="sin_bf")
+        nc.scalar.dma_start(out=cos_bf[:, 0:3, :], in_=cos1.rearrange("(p j) c -> p j c", j=3))
+        nc.scalar.dma_start(out=sin_bf[:, 0:3, :], in_=sin1.rearrange("(p j) c -> p j c", j=3))
+        nc.scalar.dma_start(out=cos_bf[:, 3, :], in_=cos2)
+        nc.scalar.dma_start(out=sin_bf[:, 3, :], in_=sin2)
+
+        w_raw = [raw.tile([P, PASSES, 4, WIDE], BF16, name="w_raw%d" % sl) for sl in range(8)]
+
+        def load_slice(sl):
+            rows = projections[sl // 2][0].rearrange("(g q t) c -> g q t c", g=PASSES, t=4)
+            first = WIDE * (sl % 2)
+            for g in range(PASSES):
+                nc.sync.dma_start(out=w_raw[sl][:, g, :, :], in_=rows[g, :, :, first : first + WIDE])
+
+        x1_raw = [raw.tile([P, 3, D], BF16, name="x1_raw%d" % b) for b in range(4)]
+        x2_raw = raw.tile([P, 4, D], BF16, name="x2_raw")
+        load_slice(0)
+        for b in range(4):
+            nc.sync.dma_start(out=x1_raw[b][:], in_=x_1[b].rearrange("(p j) k -> p j k", j=3))
+        load_slice(1)
+        nc.sync.dma_start(out=x2_raw[:], in_=x_2.rearrange("b p k -> p b k"))
+        for sl in range(2, 8):
+            load_slice(sl)
+
+        bias_f32 = const.tile([P, P], F32, name="bias_f32")
+        nc.gpsimd.tensor_copy(out=bias_f32[:], in_=bias_rows[:])
+        cos_tab = const.tile([P, 4, P], F32, name="cos_tab")
+        nc.gpsimd.tensor_copy(out=cos_tab[:], in_=cos_bf[:])
+        sin_tab = const.tile([P, 4, P], F32, name="sin_tab")
+        sin_bf_pairs = sin_bf[:].rearrange("p s (j e) -> p s j e", e=2)
+        sin_pairs = sin_tab[:].rearrange("p s (j e) -> p s j e", e=2)
+        nc.gpsimd.tensor_scalar(
+            out=sin_pairs[:, :, :, 0], in0=sin_bf_pairs[:, :, :, 0], scalar1=-1.0, scalar2=0.0, op0=MULT, op1=ADD
+        )
+        nc.gpsimd.tensor_copy(out=sin_pairs[:, :, :, 1], in_=sin_bf_pairs[:, :, :, 1])
+
+        x_codes = [const.tile([P, PASSES, WIDE], U32, name="x_codes%d" % g, align_bytes=64) for g in range(4)]
+        x_scales = [const.tile([P, PASSES, WIDE], U8, name="x_scales%d" % g, align_bytes=64) for g in range(4)]
+        x_grouped = {}
+
+        def transpose_x(grp, copy):
+            x_grouped[grp] = x_grouped_pool.tile([P, PASSES, WIDE, 4], BF16, name="x_grouped", align_bytes=64)
+            words = x_grouped[grp][:].bitcast(F32)
+            for tl in range(4):
+                tile_no = 4 * grp + tl
+                if grp < 3:
+                    tokens = x1_raw[tile_no // 3][:, tile_no % 3, :].bitcast(F32)
+                else:
+                    tokens = x2_raw[:, tl, :].bitcast(F32)
+                bank = mx_banks.tile([P, WIDE], F32, name="mx_bank")
+                for m in range(2 * PASSES):
+                    first = 2 * P * (m // 2) + m % 2
+                    nc.tensor.transpose(
+                        bank[:, P * m : P * m + P], tokens[:, first : 2 * P * (m // 2 + 1) : 2], ident[:]
+                    )
+                copy(
+                    out=words[:, :, P * tl : P * tl + P, :],
+                    in_=bank[:].rearrange("p (g u t) -> p g t u", g=PASSES, u=2),
+                )
+
+        def quantise_x(grp):
+            nc.vector.quantize_mx(
+                out=x_codes[grp][:].rearrange("p g t -> p (g t)").bitcast(FP8X4),
+                scales=x_scales[grp][:].rearrange("p g t -> p (g t)"),
+                in_=x_grouped[grp][:].rearrange("p g t k -> p (g t k)"),
+            )
+
+        w_grouped = {}
+        w_codes = {}
+
+        def regroup_w(sl, g, copy):
+            if g == 0:
+                w_grouped[sl] = w_grouped_pool.tile([P, PASSES, WIDE, 4], BF16, name="w_grouped", align_bytes=64)
+            copy(
+                out=w_grouped[sl][:, g, :, :].rearrange("p (c i) t -> p c t i", i=4),
+                in_=w_raw[sl][:, g, :, :].rearrange("p t (c i) -> p c t i", i=4),
+            )
+
+        def quantise_w(sl):
+            codes = w_codes_pool.tile([P, PASSES, WIDE], U32, name="w_code_words", align_bytes=64)
+            scales = w_codes_pool.tile([P, PASSES, WIDE], U8, name="w_scales", align_bytes=64)
+            nc.vector.quantize_mx(
+                out=codes[:].rearrange("p g c -> p (g c)").bitcast(FP8X4),
+                scales=scales[:].rearrange("p g c -> p (g c)"),
+                in_=w_grouped[sl][:].rearrange("p g c t -> p (g c t)"),
+            )
+            w_codes[sl] = (codes, scales)
+
+        bias_cols = const.tile([P, 32], F32, name="bias_cols")
+        biased = {}
+
+        def project(r):
+            sl, grp = rounds[r]
+            codes, scales = w_codes[sl]
+            biased[r] = []
+            for hh in range(4):
+                bank = mx_banks.tile([P, WIDE], F32, name="mx_bank")
+                for g in range(PASSES):
+                    nc.tensor.matmul_mx(
+                        out=bank[:],
+                        lhsT=codes[:, g, P * hh : P * hh + P].bitcast(FP8X4),
+                        lhsT_scale=scales[:, g, P * hh : P * hh + P],
+                        rhs=x_codes[grp][:, g, :].bitcast(FP8X4),
+                        rhs_scale=x_scales[grp][:, g, :],
+                        start=(g == 0),
+                        stop=(g == PASSES - 1),
+                    )
+                t = biased_pool.tile([P, WIDE], F32, name="biased")
+                col = 4 * sl + hh
+                nc.scalar.activation(
+                    out=t[:], in_=bank[:], func=IDENTITY, bias=bias_cols[:, col : col + 1],
+                    scale=projections[sl // 2][3],
+                )
+                biased[r].append(t)
+
+        back = {}
+
+        def transpose_back(r):
+            back[r] = []
+            for tl in range(4):
+                bank = back_banks.tile([P, WIDE], F32, name="back_bank")
+                for hh in range(4):
+                    nc.tensor.transpose(bank[:, P * hh : P * hh + P], biased[r][hh][:, P * tl : P * tl + P], ident[:])
+                back[r].append(bank)
+
+        y1_open = {}
+
+        def rope(r):
+            sl, grp = rounds[r]
+            heads = projections[sl // 2][2][:, 4 * (sl % 2) : 4 * (sl % 2) + 4, :, :]
+            for tl in range(4):
+                tile_no = 4 * grp + tl
+                slot = tile_no % 3 if grp < 3 else 3
+                bank = back[r][tl]
+                by_cos = products_pool.tile([P, 4, P], F32, name="by_cos")
+                nc.vector.tensor_tensor(
+                    out=by_cos[:],
+                    in0=bank[:].rearrange("p (h c) -> p h c", h=4),
+                    in1=cos_tab[:, slot, :].unsqueeze(1).to_broadcast([P, 4, P]),
+                    op=MULT,
+                )
+                by_sin = products_pool.tile([P, 4, P], F32, name="by_sin")
+                nc.vector.tensor_tensor(
+                    out=by_sin[:].rearrange("p h (j e) -> p h j e", e=2),
+                    in0=bank[:].rearrange("p (h j e) -> p h j e", h=4, e=2)[:, :, :, ::-1],
+                    in1=sin_pairs[:, slot, :, :].unsqueeze(1).to_broadcast([P, 4, P // 2, 2]),
+                    op=MULT,
+                )
+                if grp < 3:
+                    b, j = tile_no // 3, tile_no % 3
+                    if j == 0:
+                        y1_open[b] = y1_pool.tile([P, 4, 3, P], F32, name="y1")
+                    y = y1_open[b]
+                    nc.gpsimd.tensor_tensor(out=y[:, :, j, :], in0=by_cos[:], in1=by_sin[:], op=ADD)
+                    if j == 2:
+                        nc.sync.dma_start(
+                            out=heads[b, :, 0:N1, :].rearrange("h (p j) c -> p h (j c)", j=3),
+                            in_=y[:].rearrange("p h j c -> p h (j c)"),
+                        )
+                else:
+                    y = y2_pool.tile([P, 4, P], F32, name="y2")
+                    nc.gpsimd.tensor_tensor(out=y[:], in0=by_cos[:], in1=by_sin[:], op=ADD)
+                    nc.sync.dma_start(out=heads[tl, :, N1:WIDE, :].rearrange("h p c -> p h c"), in_=y[:])
+
+        for g in range(PASSES):
+            regroup_w(0, g, nc.vector.tensor_copy)
+        quantise_w(0)
+        transpose_x(0, nc.scalar.copy)
+        quantise_x(0)
+        bias_bank = back_banks.tile([P, WIDE], F32, name="back_bank")
+        nc.tensor.transpose(bias_bank[:, 0:P], bias_f32[:], ident[:])
+        for w in range(4):
+            nc.scalar.mul(
+                out=bias_cols[:, 8 * w : 8 * w + 8], in_=bias_bank[:, 8 * w : 8 * w + 8], mul=projections[w][3]
+            )
+        transpose_x(1, nc.vector.tensor_copy)
+        project(0)
+        quantise_x(1)
+
+        for i in range(n_rounds):
+            transpose_back(i)
+            if i < 14:
+                regroup_w(1 + i // 2, i % 2, nc.scalar.copy)
+            if i < 2:
+                transpose_x(2 + i, nc.scalar.copy)
+            if i + 1 < n_rounds:
+                project(i + 1)
+            rope(i)
+            if i < 2:
+                quantise_x(2 + i)
+            if i < 14 and i % 2 == 1:
+                quantise_w(1 + i // 2)

@@ -98,25 +98,25 @@ def tile_dualmultiheadattention_pa_kernel(
         x_scales = [const.tile([P, PASSES, WIDE], U8, name="x_scales%d" % g, align_bytes=64) for g in range(4)]
         x_grouped = {}
 
-        def transpose_x(grp, copy):
-            x_grouped[grp] = x_grouped_pool.tile([P, PASSES, WIDE, 4], BF16, name="x_grouped", align_bytes=64)
+        def transpose_x(grp, tl, copy):
+            if tl == 0:
+                x_grouped[grp] = x_grouped_pool.tile([P, PASSES, WIDE, 4], BF16, name="x_grouped", align_bytes=64)
             words = x_grouped[grp][:].bitcast(F32)
-            for tl in range(4):
-                tile_no = 4 * grp + tl
-                if grp < 3:
-                    tokens = x1_raw[tile_no // 3][:, tile_no % 3, :].bitcast(F32)
-                else:
-                    tokens = x2_raw[:, tl, :].bitcast(F32)
-                bank = mx_banks.tile([P, WIDE], F32, name="mx_bank")
-                for m in range(2 * PASSES):
-                    first = 2 * P * (m // 2) + m % 2
-                    nc.tensor.transpose(
-                        bank[:, P * m : P * m + P], tokens[:, first : 2 * P * (m // 2 + 1) : 2], ident[:]
-                    )
-                copy(
-                    out=words[:, :, P * tl : P * tl + P, :],
-                    in_=bank[:].rearrange("p (g u t) -> p g t u", g=PASSES, u=2),
+            tile_no = 4 * grp + tl
+            if grp < 3:
+                tokens = x1_raw[tile_no // 3][:, tile_no % 3, :].bitcast(F32)
+            else:
+                tokens = x2_raw[:, tl, :].bitcast(F32)
+            bank = mx_banks.tile([P, WIDE], F32, name="mx_bank")
+            for m in range(2 * PASSES):
+                first = 2 * P * (m // 2) + m % 2
+                nc.tensor.transpose(
+                    bank[:, P * m : P * m + P], tokens[:, first : 2 * P * (m // 2 + 1) : 2], ident[:]
                 )
+            copy(
+                out=words[:, :, P * tl : P * tl + P, :],
+                in_=bank[:].rearrange("p (g u t) -> p g t u", g=PASSES, u=2),
+            )
 
         def quantise_x(grp):
             nc.vector.quantize_mx(
@@ -128,12 +128,12 @@ def tile_dualmultiheadattention_pa_kernel(
         w_grouped = {}
         w_codes = {}
 
-        def regroup_w(sl, g, copy):
-            if g == 0:
+        def regroup_w(sl, g, first, last, copy):
+            if g == 0 and first == 0:
                 w_grouped[sl] = w_grouped_pool.tile([P, PASSES, WIDE, 4], BF16, name="w_grouped", align_bytes=64)
             copy(
-                out=w_grouped[sl][:, g, :, :].rearrange("p (c i) t -> p c t i", i=4),
-                in_=w_raw[sl][:, g, :, :].rearrange("p t (c i) -> p c t i", i=4),
+                out=w_grouped[sl][:, g, first:last, :].rearrange("p (c i) t -> p c t i", i=4),
+                in_=w_raw[sl][:, g, :, first:last].rearrange("p t (c i) -> p c t i", i=4),
             )
 
         def quantise_w(sl):
@@ -149,83 +149,79 @@ def tile_dualmultiheadattention_pa_kernel(
         bias_cols = const.tile([P, 32], F32, name="bias_cols")
         biased = {}
 
-        def project(r):
+        def project(r, hh):
             sl, grp = rounds[r]
             codes, scales = w_codes[sl]
-            biased[r] = []
-            for hh in range(4):
-                bank = mx_banks.tile([P, WIDE], F32, name="mx_bank")
-                for g in range(PASSES):
-                    nc.tensor.matmul_mx(
-                        out=bank[:],
-                        lhsT=codes[:, g, P * hh : P * hh + P].bitcast(FP8X4),
-                        lhsT_scale=scales[:, g, P * hh : P * hh + P],
-                        rhs=x_codes[grp][:, g, :].bitcast(FP8X4),
-                        rhs_scale=x_scales[grp][:, g, :],
-                        start=(g == 0),
-                        stop=(g == PASSES - 1),
-                    )
-                t = biased_pool.tile([P, WIDE], F32, name="biased")
-                col = 4 * sl + hh
-                nc.scalar.activation(
-                    out=t[:], in_=bank[:], func=IDENTITY, bias=bias_cols[:, col : col + 1],
-                    scale=projections[sl // 2][3],
+            bank = mx_banks.tile([P, WIDE], F32, name="mx_bank")
+            for g in range(PASSES):
+                nc.tensor.matmul_mx(
+                    out=bank[:],
+                    lhsT=codes[:, g, P * hh : P * hh + P].bitcast(FP8X4),
+                    lhsT_scale=scales[:, g, P * hh : P * hh + P],
+                    rhs=x_codes[grp][:, g, :].bitcast(FP8X4),
+                    rhs_scale=x_scales[grp][:, g, :],
+                    start=(g == 0),
+                    stop=(g == PASSES - 1),
                 )
-                biased[r].append(t)
+            t = biased_pool.tile([P, WIDE], F32, name="biased")
+            col = 4 * sl + hh
+            nc.scalar.activation(
+                out=t[:], in_=bank[:], func=IDENTITY, bias=bias_cols[:, col : col + 1],
+                scale=projections[sl // 2][3],
+            )
+            biased[r, hh] = t
 
         back = {}
 
-        def transpose_back(r):
-            back[r] = []
-            for tl in range(4):
-                bank = back_banks.tile([P, WIDE], F32, name="back_bank")
-                for hh in range(4):
-                    nc.tensor.transpose(bank[:, P * hh : P * hh + P], biased[r][hh][:, P * tl : P * tl + P], ident[:])
-                back[r].append(bank)
+        def transpose_back(r, tl):
+            bank = back_banks.tile([P, WIDE], F32, name="back_bank")
+            for hh in range(4):
+                nc.tensor.transpose(bank[:, P * hh : P * hh + P], biased[r, hh][:, P * tl : P * tl + P], ident[:])
+            back[r, tl] = bank
 
         y1_open = {}
 
-        def rope(r):
+        def rope(r, tl):
             sl, grp = rounds[r]
             heads = projections[sl // 2][2][:, 4 * (sl % 2) : 4 * (sl % 2) + 4, :, :]
-            for tl in range(4):
-                tile_no = 4 * grp + tl
-                slot = tile_no % 3 if grp < 3 else 3
-                bank = back[r][tl]
-                by_cos = products_pool.tile([P, 4, P], F32, name="by_cos")
-                nc.vector.tensor_tensor(
-                    out=by_cos[:],
-                    in0=bank[:].rearrange("p (h c) -> p h c", h=4),
-                    in1=cos_tab[:, slot, :].unsqueeze(1).to_broadcast([P, 4, P]),
-                    op=MULT,
-                )
-                by_sin = products_pool.tile([P, 4, P], F32, name="by_sin")
-                nc.vector.tensor_tensor(
-                    out=by_sin[:].rearrange("p h (j e) -> p h j e", e=2),
-                    in0=bank[:].rearrange("p (h j e) -> p h j e", h=4, e=2)[:, :, :, ::-1],
-                    in1=sin_pairs[:, slot, :, :].unsqueeze(1).to_broadcast([P, 4, P // 2, 2]),
-                    op=MULT,
-                )
-                if grp < 3:
-                    b, j = tile_no // 3, tile_no % 3
-                    if j == 0:
-                        y1_open[b] = y1_pool.tile([P, 4, 3, P], F32, name="y1")
-                    y = y1_open[b]
-                    nc.gpsimd.tensor_tensor(out=y[:, :, j, :], in0=by_cos[:], in1=by_sin[:], op=ADD)
-                    if j == 2:
-                        nc.sync.dma_start(
-                            out=heads[b, :, 0:N1, :].rearrange("h (p j) c -> p h (j c)", j=3),
-                            in_=y[:].rearrange("p h j c -> p h (j c)"),
-                        )
-                else:
-                    y = y2_pool.tile([P, 4, P], F32, name="y2")
-                    nc.gpsimd.tensor_tensor(out=y[:], in0=by_cos[:], in1=by_sin[:], op=ADD)
-                    nc.sync.dma_start(out=heads[tl, :, N1:WIDE, :].rearrange("h p c -> p h c"), in_=y[:])
+            tile_no = 4 * grp + tl
+            slot = tile_no % 3 if grp < 3 else 3
+            bank = back[r, tl]
+            by_cos = products_pool.tile([P, 4, P], F32, name="by_cos")
+            nc.vector.tensor_tensor(
+                out=by_cos[:],
+                in0=bank[:].rearrange("p (h c) -> p h c", h=4),
+                in1=cos_tab[:, slot, :].unsqueeze(1).to_broadcast([P, 4, P]),
+                op=MULT,
+            )
+            by_sin = products_pool.tile([P, 4, P], F32, name="by_sin")
+            nc.vector.tensor_tensor(
+                out=by_sin[:].rearrange("p h (j e) -> p h j e", e=2),
+                in0=bank[:].rearrange("p (h j e) -> p h j e", h=4, e=2)[:, :, :, ::-1],
+                in1=sin_pairs[:, slot, :, :].unsqueeze(1).to_broadcast([P, 4, P // 2, 2]),
+                op=MULT,
+            )
+            if grp < 3:
+                b, j = tile_no // 3, tile_no % 3
+                if j == 0:
+                    y1_open[b] = y1_pool.tile([P, 4, 3, P], F32, name="y1")
+                y = y1_open[b]
+                nc.gpsimd.tensor_tensor(out=y[:, :, j, :], in0=by_cos[:], in1=by_sin[:], op=ADD)
+                if j == 2:
+                    nc.sync.dma_start(
+                        out=heads[b, :, 0:N1, :].rearrange("h (p j) c -> p h (j c)", j=3),
+                        in_=y[:].rearrange("p h j c -> p h (j c)"),
+                    )
+            else:
+                y = y2_pool.tile([P, 4, P], F32, name="y2")
+                nc.gpsimd.tensor_tensor(out=y[:], in0=by_cos[:], in1=by_sin[:], op=ADD)
+                nc.sync.dma_start(out=heads[tl, :, N1:WIDE, :].rearrange("h p c -> p h c"), in_=y[:])
 
         for g in range(PASSES):
-            regroup_w(0, g, nc.vector.tensor_copy)
+            regroup_w(0, g, 0, WIDE, nc.vector.tensor_copy)
         quantise_w(0)
-        transpose_x(0, nc.scalar.copy)
+        for tl in range(4):
+            transpose_x(0, tl, nc.scalar.copy)
         quantise_x(0)
         bias_bank = back_banks.tile([P, WIDE], F32, name="back_bank")
         nc.tensor.transpose(bias_bank[:, 0:P], bias_f32[:], ident[:])
@@ -233,20 +229,24 @@ def tile_dualmultiheadattention_pa_kernel(
             nc.scalar.mul(
                 out=bias_cols[:, 8 * w : 8 * w + 8], in_=bias_bank[:, 8 * w : 8 * w + 8], mul=projections[w][3]
             )
-        transpose_x(1, nc.vector.tensor_copy)
-        project(0)
+        for tl in range(4):
+            transpose_x(1, tl, nc.vector.tensor_copy)
+        for hh in range(4):
+            project(0, hh)
         quantise_x(1)
 
+        x_group_of_round = {0: 2, 4: 3}
         for i in range(n_rounds):
-            transpose_back(i)
-            if i < 14:
-                regroup_w(1 + i // 2, i % 2, nc.scalar.copy)
-            if i < 2:
-                transpose_x(2 + i, nc.scalar.copy)
-            if i + 1 < n_rounds:
-                project(i + 1)
-            rope(i)
-            if i < 2:
-                quantise_x(2 + i)
+            for c in range(4):
+                if i + 1 < n_rounds:
+                    project(i + 1, c)
+                transpose_back(i, c)
+                if i in x_group_of_round:
+                    transpose_x(x_group_of_round[i], c, nc.scalar.copy)
+                if i < 14:
+                    regroup_w(1 + i // 2, i % 2, P * c, P * c + P, nc.scalar.copy)
+                rope(i, c)
+            if i in x_group_of_round:
+                quantise_x(x_group_of_round[i])
             if i < 14 and i % 2 == 1:
                 quantise_w(1 + i // 2)

@@ -26,13 +26,14 @@ def tile_dualmultiheadattention_pa_kernel(
 ):
     nc = tc.nc
     projections = [
-        (wq1, bq1, out_0, Q_SCALE, (0, 1, 2)),
-        (wk1, bk1, out_1, 1.0, (0, 1, 2)),
-        (wq2, bq2, out_0, Q_SCALE, (3,)),
-        (wk2, bk2, out_1, 1.0, (3,)),
+        (wq1, bq1, out_0, Q_SCALE, (0, 1, 2, 3)),
+        (wk1, bk1, out_1, 1.0, (0, 1, 2, 3)),
+        (wq2, bq2, out_0, Q_SCALE, (4,)),
+        (wk2, bk2, out_1, 1.0, (4,)),
     ]
-    rounds = [(sl, grp) for sl in range(8) for grp in projections[sl // 2][4]]
-    n_rounds = len(rounds)
+    units = [(sl, grp, hh) for sl in range(8) for grp in projections[sl // 2][4] for hh in range(4)]
+    n_units = len(units)
+    group_tiles = [3, 3, 3, 3, 4]
 
     with ExitStack() as ctx:
         const = ctx.enter_context(tc.tile_pool(name="const", bufs=1))
@@ -40,30 +41,23 @@ def tile_dualmultiheadattention_pa_kernel(
         x_grouped_pool = ctx.enter_context(tc.tile_pool(name="x_grouped", bufs=2))
         w_grouped_pool = ctx.enter_context(tc.tile_pool(name="w_grouped", bufs=2))
         w_codes_pool = ctx.enter_context(tc.tile_pool(name="w_codes", bufs=4))
-        biased_pool = ctx.enter_context(tc.tile_pool(name="biased", bufs=8))
+        biased_pool = ctx.enter_context(tc.tile_pool(name="biased", bufs=3))
+        turned_pool = ctx.enter_context(tc.tile_pool(name="turned", bufs=3))
         products_pool = ctx.enter_context(tc.tile_pool(name="products", bufs=3))
-        y1_pool = ctx.enter_context(tc.tile_pool(name="y1", bufs=3))
-        y2_pool = ctx.enter_context(tc.tile_pool(name="y2", bufs=3))
+        y_pool = ctx.enter_context(tc.tile_pool(name="y", bufs=4))
         mx_banks = ctx.enter_context(tc.psum_pool(name="mx_banks", bufs=3))
         back_banks = ctx.enter_context(tc.psum_pool(name="back_banks", bufs=5))
         ctx.enter_context(tc.manual_schedule())
 
         ident = const.tile([P, P], F32, name="ident")
         masks.make_identity(nc, ident[:])
+        one_column = const.tile([P, 1], F32, name="one_column")
+        nc.vector.memset(one_column[:], 0.0)
+        table_loaded = const.tile([P, 1], F32, name="table_loaded")
+        nc.scalar.activation(out=table_loaded[:], in_=one_column[:], func=IDENTITY, bias=one_column[:], scale=1.0)
 
         bias_rows = const.tile([P, P], BF16, name="bias_rows")
         nc.vector.memset(bias_rows[:], 0.0)
-        for w in range(4):
-            nc.scalar.dma_start(
-                out=bias_rows[8 * w : 8 * w + 8, :], in_=projections[w][1].rearrange("(h c) -> h c", c=P)
-            )
-        cos_bf = const.tile([P, 4, P], BF16, name="cos_bf")
-        sin_bf = const.tile([P, 4, P], BF16, name="sin_bf")
-        nc.scalar.dma_start(out=cos_bf[:, 0:3, :], in_=cos1.rearrange("(p j) c -> p j c", j=3))
-        nc.scalar.dma_start(out=sin_bf[:, 0:3, :], in_=sin1.rearrange("(p j) c -> p j c", j=3))
-        nc.scalar.dma_start(out=cos_bf[:, 3, :], in_=cos2)
-        nc.scalar.dma_start(out=sin_bf[:, 3, :], in_=sin2)
-
         w_raw = [raw.tile([P, PASSES, 4, WIDE], BF16, name="w_raw%d" % sl) for sl in range(8)]
 
         def load_slice(sl):
@@ -72,42 +66,71 @@ def tile_dualmultiheadattention_pa_kernel(
             for g in range(PASSES):
                 nc.sync.dma_start(out=w_raw[sl][:, g, :, :], in_=rows[g, :, :, first : first + WIDE])
 
-        x1_raw = [raw.tile([P, 3, D], BF16, name="x1_raw%d" % b) for b in range(4)]
-        x2_raw = raw.tile([P, 4, D], BF16, name="x2_raw")
+        x_raw = [raw.tile([P, group_tiles[g], D], BF16, name="x_raw%d" % g) for g in range(5)]
+
+        def load_x1(b):
+            nc.sync.dma_start(out=x_raw[b][:], in_=x_1[b].rearrange("(p j) k -> p j k", j=3))
+
+        cos_bf = const.tile([P, 4, P], BF16, name="cos_bf")
+        sin_bf = const.tile([P, 4, P], BF16, name="sin_bf")
         load_slice(0)
-        for b in range(4):
-            nc.sync.dma_start(out=x1_raw[b][:], in_=x_1[b].rearrange("(p j) k -> p j k", j=3))
+        load_x1(0)
+        for w in range(4):
+            nc.sync.dma_start(
+                out=bias_rows[8 * w : 8 * w + 8, :], in_=projections[w][1].rearrange("(h c) -> h c", c=P)
+            )
+        nc.sync.dma_start(out=cos_bf[:, 0:3, :], in_=cos1.rearrange("(p j) c -> p j c", j=3))
+        nc.sync.dma_start(out=sin_bf[:, 0:3, :], in_=sin1.rearrange("(p j) c -> p j c", j=3))
+        nc.sync.dma_start(out=cos_bf[:, 3, :], in_=cos2)
+        nc.sync.dma_start(out=sin_bf[:, 3, :], in_=sin2)
+        load_x1(1)
+        load_x1(2)
         load_slice(1)
-        nc.sync.dma_start(out=x2_raw[:], in_=x_2.rearrange("b p k -> p b k"))
-        for sl in range(2, 8):
+        load_x1(3)
+        load_slice(2)
+        nc.sync.dma_start(out=x_raw[4][:], in_=x_2.rearrange("b p k -> p b k"))
+        for sl in range(3, 8):
             load_slice(sl)
 
+        def widen(out, in_, factor):
+            nc.gpsimd.tensor_scalar(out=out, in0=in_, scalar1=factor, scalar2=0.0, op0=MULT, op1=ADD)
+
         bias_f32 = const.tile([P, P], F32, name="bias_f32")
-        nc.gpsimd.tensor_copy(out=bias_f32[:], in_=bias_rows[:])
+        widen(bias_f32[:], bias_rows[:], 1.0)
+        swap = const.tile([P, P], F32, name="swap")
+        swap_pairs = swap[:].rearrange("p (j e) -> p j e", e=2)
+        ident_pairs = ident[:].rearrange("p (j e) -> p j e", e=2)
+        for e in range(2):
+            widen(swap_pairs[:, :, e], ident_pairs[:, :, 1 - e], 1.0)
         cos_tab = const.tile([P, 4, P], F32, name="cos_tab")
-        nc.gpsimd.tensor_copy(out=cos_tab[:], in_=cos_bf[:])
+        widen(cos_tab[:], cos_bf[:], 1.0)
         sin_tab = const.tile([P, 4, P], F32, name="sin_tab")
+        sin_src = const.tile([P, 4, P], F32, name="sin_src")
         sin_bf_pairs = sin_bf[:].rearrange("p s (j e) -> p s j e", e=2)
         sin_pairs = sin_tab[:].rearrange("p s (j e) -> p s j e", e=2)
-        nc.gpsimd.tensor_scalar(
-            out=sin_pairs[:, :, :, 0], in0=sin_bf_pairs[:, :, :, 0], scalar1=-1.0, scalar2=0.0, op0=MULT, op1=ADD
-        )
-        nc.gpsimd.tensor_copy(out=sin_pairs[:, :, :, 1], in_=sin_bf_pairs[:, :, :, 1])
+        sin_src_pairs = sin_src[:].rearrange("p s (j e) -> p s j e", e=2)
+        for pairs, crossed in ((sin_src_pairs, 1), (sin_pairs, 0)):
+            widen(pairs[:, :, :, crossed], sin_bf_pairs[:, :, :, 0], -1.0)
+            widen(pairs[:, :, :, 1 - crossed], sin_bf_pairs[:, :, :, 1], 1.0)
+        cos_feat = const.tile([P, 4, P], F32, name="cos_feat")
+        sin_feat = const.tile([P, 4, P], F32, name="sin_feat")
 
-        x_codes = [const.tile([P, PASSES, WIDE], U32, name="x_codes%d" % g, align_bytes=64) for g in range(4)]
-        x_scales = [const.tile([P, PASSES, WIDE], U8, name="x_scales%d" % g, align_bytes=64) for g in range(4)]
+        x_codes = [
+            const.tile([P, PASSES, P * group_tiles[g]], U32, name="x_codes%d" % g, align_bytes=64) for g in range(5)
+        ]
+        x_scales = [
+            const.tile([P, PASSES, P * group_tiles[g]], U8, name="x_scales%d" % g, align_bytes=64) for g in range(5)
+        ]
         x_grouped = {}
 
         def transpose_x(grp, tl, copy):
             if tl == 0:
-                x_grouped[grp] = x_grouped_pool.tile([P, PASSES, WIDE, 4], BF16, name="x_grouped", align_bytes=64)
+                x_grouped[grp] = x_grouped_pool.tile(
+                    [P, PASSES, P * group_tiles[grp], 4], BF16, name="x_grouped", align_bytes=64
+                )
             words = x_grouped[grp][:].bitcast(F32)
-            tile_no = 4 * grp + tl
-            if grp < 3:
-                tokens = x1_raw[tile_no // 3][:, tile_no % 3, :].bitcast(F32)
-            else:
-                tokens = x2_raw[:, tl, :].bitcast(F32)
-            bank = mx_banks.tile([P, WIDE], F32, name="mx_bank")
+            tokens = x_raw[grp][:, tl, :].bitcast(F32)
+            bank = back_banks.tile([P, WIDE], F32, name="back_bank")
             for m in range(2 * PASSES):
                 first = 2 * P * (m // 2) + m % 2
                 nc.tensor.transpose(
@@ -118,12 +141,23 @@ def tile_dualmultiheadattention_pa_kernel(
                 in_=bank[:].rearrange("p (g u t) -> p g t u", g=PASSES, u=2),
             )
 
+        def quantise(codes, scales, grouped):
+            words = codes[:].rearrange("p g c -> p (g c)")
+            planes = scales[:].rearrange("p g c -> p (g c)")
+            values = grouped[:].rearrange("p g c t -> p (g c t)")
+            count = words.shape[1]
+            first = 0
+            for width in (1024, 512, 256):
+                if count - first >= width:
+                    nc.vector.quantize_mx(
+                        out=words[:, first : first + width].bitcast(FP8X4),
+                        scales=planes[:, first : first + width],
+                        in_=values[:, 4 * first : 4 * (first + width)],
+                    )
+                    first += width
+
         def quantise_x(grp):
-            nc.vector.quantize_mx(
-                out=x_codes[grp][:].rearrange("p g t -> p (g t)").bitcast(FP8X4),
-                scales=x_scales[grp][:].rearrange("p g t -> p (g t)"),
-                in_=x_grouped[grp][:].rearrange("p g t k -> p (g t k)"),
-            )
+            quantise(x_codes[grp], x_scales[grp], x_grouped[grp])
 
         w_grouped = {}
         w_codes = {}
@@ -139,114 +173,173 @@ def tile_dualmultiheadattention_pa_kernel(
         def quantise_w(sl):
             codes = w_codes_pool.tile([P, PASSES, WIDE], U32, name="w_code_words", align_bytes=64)
             scales = w_codes_pool.tile([P, PASSES, WIDE], U8, name="w_scales", align_bytes=64)
-            nc.vector.quantize_mx(
-                out=codes[:].rearrange("p g c -> p (g c)").bitcast(FP8X4),
-                scales=scales[:].rearrange("p g c -> p (g c)"),
-                in_=w_grouped[sl][:].rearrange("p g c t -> p (g c t)"),
-            )
+            quantise(codes, scales, w_grouped[sl])
             w_codes[sl] = (codes, scales)
 
         bias_cols = const.tile([P, 32], F32, name="bias_cols")
-        biased = {}
+        bias_raw = const.tile([P, 32], F32, name="bias_raw")
+        mx_bank_of = {}
 
-        def project(r, hh):
-            sl, grp = rounds[r]
+        def project(u):
+            sl, grp, hh = units[u]
             codes, scales = w_codes[sl]
             bank = mx_banks.tile([P, WIDE], F32, name="mx_bank")
-            for g in range(PASSES):
-                nc.tensor.matmul_mx(
-                    out=bank[:],
-                    lhsT=codes[:, g, P * hh : P * hh + P].bitcast(FP8X4),
-                    lhsT_scale=scales[:, g, P * hh : P * hh + P],
-                    rhs=x_codes[grp][:, g, :].bitcast(FP8X4),
-                    rhs_scale=x_scales[grp][:, g, :],
-                    start=(g == 0),
-                    stop=(g == PASSES - 1),
-                )
+            for first, count in ((0, 256), (256, 128)) if grp < 4 else ((0, 512),):
+                for g in range(PASSES):
+                    nc.tensor.matmul_mx(
+                        out=bank[:, first : first + count],
+                        lhsT=codes[:, g, P * hh : P * hh + P].bitcast(FP8X4),
+                        lhsT_scale=scales[:, g, P * hh : P * hh + P],
+                        rhs=x_codes[grp][:, g, first : first + count].bitcast(FP8X4),
+                        rhs_scale=x_scales[grp][:, g, first : first + count],
+                        start=(g == 0),
+                        stop=(g == PASSES - 1),
+                    )
+            mx_bank_of[u] = bank
+
+        def table_of(u, table):
+            if units[u][1] < 4:
+                return table[:, 0:3, :]
+            return table[:, 3, :].unsqueeze(1).to_broadcast([P, 4, P])
+
+        def tiles_of(u):
+            return group_tiles[units[u][1]]
+
+        biased = {}
+
+        def add_bias(u):
+            sl, grp, hh = units[u]
+            n = P * tiles_of(u)
             t = biased_pool.tile([P, WIDE], F32, name="biased")
             col = 4 * sl + hh
             nc.scalar.activation(
-                out=t[:], in_=bank[:], func=IDENTITY, bias=bias_cols[:, col : col + 1],
+                out=t[:, 0:n], in_=mx_bank_of[u][:, 0:n], func=IDENTITY, bias=bias_cols[:, col : col + 1],
                 scale=projections[sl // 2][3],
             )
-            biased[r, hh] = t
+            biased[u] = t
 
         back = {}
 
-        def transpose_back(r, tl):
+        def transpose_back(u):
             bank = back_banks.tile([P, WIDE], F32, name="back_bank")
-            for hh in range(4):
-                nc.tensor.transpose(bank[:, P * hh : P * hh + P], biased[r, hh][:, P * tl : P * tl + P], ident[:])
-            back[r, tl] = bank
+            for tl in range(tiles_of(u)):
+                cols = slice(P * tl, P * tl + P)
+                nc.tensor.transpose(bank[:, cols], biased[u][:, cols], ident[:])
+            back[u] = bank
 
-        y1_open = {}
+        turned = {}
 
-        def rope(r, tl):
-            sl, grp = rounds[r]
-            heads = projections[sl // 2][2][:, 4 * (sl % 2) : 4 * (sl % 2) + 4, :, :]
-            tile_no = 4 * grp + tl
-            slot = tile_no % 3 if grp < 3 else 3
-            bank = back[r, tl]
-            by_cos = products_pool.tile([P, 4, P], F32, name="by_cos")
-            nc.vector.tensor_tensor(
-                out=by_cos[:],
-                in0=bank[:].rearrange("p (h c) -> p h c", h=4),
-                in1=cos_tab[:, slot, :].unsqueeze(1).to_broadcast([P, 4, P]),
-                op=MULT,
-            )
-            by_sin = products_pool.tile([P, 4, P], F32, name="by_sin")
-            nc.vector.tensor_tensor(
-                out=by_sin[:].rearrange("p h (j e) -> p h j e", e=2),
-                in0=bank[:].rearrange("p (h j e) -> p h j e", h=4, e=2)[:, :, :, ::-1],
-                in1=sin_pairs[:, slot, :, :].unsqueeze(1).to_broadcast([P, 4, P // 2, 2]),
-                op=MULT,
-            )
-            if grp < 3:
-                b, j = tile_no // 3, tile_no % 3
-                if j == 0:
-                    y1_open[b] = y1_pool.tile([P, 4, 3, P], F32, name="y1")
-                y = y1_open[b]
-                nc.gpsimd.tensor_tensor(out=y[:, :, j, :], in0=by_cos[:], in1=by_sin[:], op=ADD)
-                if j == 2:
-                    nc.sync.dma_start(
-                        out=heads[b, :, 0:N1, :].rearrange("h (p j) c -> p h (j c)", j=3),
-                        in_=y[:].rearrange("p h j c -> p h (j c)"),
-                    )
+        def turn(u):
+            sl, grp, hh = units[u]
+            tiles = tiles_of(u)
+            col = 4 * sl + hh
+            turned[u] = []
+            for table, name in ((cos_feat, "turned_cos"), (sin_feat, "turned_sin")):
+                t = turned_pool.tile([P, WIDE], F32, name=name)
+                nc.vector.scalar_tensor_tensor(
+                    out=t[:, 0 : P * tiles].rearrange("p (s t) -> p s t", t=P),
+                    in0=mx_bank_of[u][:, 0 : P * tiles].rearrange("p (s t) -> p s t", t=P),
+                    scalar=bias_raw[:, col : col + 1], in1=table_of(u, table), op0=ADD, op1=MULT,
+                )
+                turned[u].append(t)
+
+        def merge_back(u):
+            bank = back_banks.tile([P, WIDE], F32, name="back_bank")
+            for tl in range(tiles_of(u)):
+                cols = slice(P * tl, P * tl + P)
+                by_cos, by_sin = turned[u]
+                nc.tensor.matmul(bank[:, cols], lhsT=by_cos[:, cols], rhs=ident[:], is_transpose=True, start=True, stop=False)
+                nc.tensor.matmul(bank[:, cols], lhsT=by_sin[:, cols], rhs=swap[:], is_transpose=True, start=False, stop=True)
+            back[u] = bank
+
+        y_of = {}
+
+        def open_y(u):
+            y = y_pool.tile([P, 2, tiles_of(u), P], F32, name="y")
+            y_of[u] = y[:, 0, :, :]
+            y_of[u + 1] = y[:, 1, :, :]
+
+        def store(u):
+            sl, grp, hh = units[u]
+            heads = projections[sl // 2][2]
+            h = 4 * (sl % 2) + hh
+            if grp < 4:
+                nc.sync.dma_start(
+                    out=heads[grp, h, 0:N1, :].rearrange("(p j) c -> p j c", j=3), in_=y_of[u]
+                )
             else:
-                y = y2_pool.tile([P, 4, P], F32, name="y2")
-                nc.gpsimd.tensor_tensor(out=y[:], in0=by_cos[:], in1=by_sin[:], op=ADD)
-                nc.sync.dma_start(out=heads[tl, :, N1:WIDE, :].rearrange("h p c -> p h c"), in_=y[:])
+                nc.sync.dma_start(out=heads[:, h, N1:WIDE, :].rearrange("b p c -> p b c"), in_=y_of[u])
+
+        def leave_merged(u):
+            nc.scalar.mul(
+                out=y_of[u], in_=back[u][:, 0 : P * tiles_of(u)].rearrange("p (s c) -> p s c", c=P),
+                mul=projections[units[u][0] // 2][3],
+            )
+            store(u)
+
+        def rope(u):
+            tiles = tiles_of(u)
+            bank = back[u]
+            by_cos = products_pool.tile([P, tiles, P], F32, name="by_cos")
+            nc.vector.tensor_tensor(
+                out=by_cos[:], in0=bank[:, 0 : P * tiles].rearrange("p (s c) -> p s c", c=P),
+                in1=table_of(u, cos_tab), op=MULT,
+            )
+            by_sin = products_pool.tile([P, tiles, P], F32, name="by_sin")
+            nc.vector.tensor_tensor(
+                out=by_sin[:].rearrange("p s (j e) -> p s j e", e=2),
+                in0=bank[:, 0 : P * tiles].rearrange("p (s j e) -> p s j e", s=tiles, e=2)[:, :, :, ::-1],
+                in1=table_of(u, sin_tab).rearrange("p s (j e) -> p s j e", e=2),
+                op=MULT,
+            )
+            nc.gpsimd.tensor_tensor(out=y_of[u], in0=by_cos[:], in1=by_sin[:], op=ADD)
+            store(u)
 
         for g in range(PASSES):
             regroup_w(0, g, 0, WIDE, nc.vector.tensor_copy)
         quantise_w(0)
-        for tl in range(4):
+        for tl in range(3):
             transpose_x(0, tl, nc.scalar.copy)
         quantise_x(0)
         bias_bank = back_banks.tile([P, WIDE], F32, name="back_bank")
         nc.tensor.transpose(bias_bank[:, 0:P], bias_f32[:], ident[:])
+        nc.scalar.copy(out=bias_raw[:], in_=bias_bank[:, 0:32])
         for w in range(4):
-            nc.scalar.mul(
-                out=bias_cols[:, 8 * w : 8 * w + 8], in_=bias_bank[:, 8 * w : 8 * w + 8], mul=projections[w][3]
-            )
-        for tl in range(4):
-            transpose_x(1, tl, nc.vector.tensor_copy)
-        for hh in range(4):
-            project(0, hh)
-        quantise_x(1)
+            nc.scalar.mul(out=bias_cols[:, 8 * w : 8 * w + 8], in_=bias_raw[:, 8 * w : 8 * w + 8], mul=projections[w][3])
+        project(0)
+        project(1)
+        add_bias(0)
+        for tab, feat in ((cos_tab, cos_feat), (sin_src, sin_feat)):
+            feat_bank = back_banks.tile([P, WIDE], F32, name="back_bank")
+            for slot in range(4):
+                nc.tensor.transpose(feat_bank[:, P * slot : P * slot + P], tab[:, slot, :], ident[:])
+            nc.scalar.copy(out=feat[:].rearrange("p s t -> p (s t)"), in_=feat_bank[:])
+        turn(1)
 
-        x_group_of_round = {0: 2, 4: 3}
-        for i in range(n_rounds):
-            for c in range(4):
-                if i + 1 < n_rounds:
-                    project(i + 1, c)
-                transpose_back(i, c)
-                if i in x_group_of_round:
-                    transpose_x(x_group_of_round[i], c, nc.scalar.copy)
-                if i < 14:
-                    regroup_w(1 + i // 2, i % 2, P * c, P * c + P, nc.scalar.copy)
-                rope(i, c)
-            if i in x_group_of_round:
-                quantise_x(x_group_of_round[i])
-            if i < 14 and i % 2 == 1:
-                quantise_w(1 + i // 2)
+        x_group_of_step = {0: (1, 0, 3), 1: (2, 0, 3), 3: (3, 0, 3), 10: (4, 0, 2), 11: (4, 2, 4)}
+        pieces = [(sl, g, c) for sl in range(1, 8) for g in range(PASSES) for c in range(4)]
+        for i in range(n_units // 2):
+            u = 2 * i
+            if u + 2 < n_units:
+                project(u + 2)
+                project(u + 3)
+                add_bias(u + 2)
+            open_y(u)
+            transpose_back(u)
+            merge_back(u + 1)
+            if i in x_group_of_step:
+                grp, tl0, tl1 = x_group_of_step[i]
+                for tl in range(tl0, tl1):
+                    transpose_x(grp, tl, nc.scalar.copy)
+            mine = pieces[7 * (i - 1) // 4 : 7 * i // 4] if i > 0 else []
+            for sl, g, c in mine:
+                regroup_w(sl, g, P * c, P * c + P, nc.scalar.copy)
+            leave_merged(u + 1)
+            if u + 2 < n_units:
+                turn(u + 3)
+            rope(u)
+            if i in x_group_of_step and tl1 == group_tiles[grp]:
+                quantise_x(grp)
+            for sl, g, c in mine:
+                if (g, c) == (PASSES - 1, 3):
+                    quantise_w(sl)

@@ -104,14 +104,11 @@ def tile_dualmultiheadattention_pa_kernel(
             widen(swap_pairs[:, :, e], ident_pairs[:, :, 1 - e], 1.0)
         cos_tab = const.tile([P, 4, P], F32, name="cos_tab")
         widen(cos_tab[:], cos_bf[:], 1.0)
-        sin_tab = const.tile([P, 4, P], F32, name="sin_tab")
         sin_src = const.tile([P, 4, P], F32, name="sin_src")
         sin_bf_pairs = sin_bf[:].rearrange("p s (j e) -> p s j e", e=2)
-        sin_pairs = sin_tab[:].rearrange("p s (j e) -> p s j e", e=2)
         sin_src_pairs = sin_src[:].rearrange("p s (j e) -> p s j e", e=2)
-        for pairs, crossed in ((sin_src_pairs, 1), (sin_pairs, 0)):
-            widen(pairs[:, :, :, crossed], sin_bf_pairs[:, :, :, 0], -1.0)
-            widen(pairs[:, :, :, 1 - crossed], sin_bf_pairs[:, :, :, 1], 1.0)
+        widen(sin_src_pairs[:, :, :, 1], sin_bf_pairs[:, :, :, 0], -1.0)
+        widen(sin_src_pairs[:, :, :, 0], sin_bf_pairs[:, :, :, 1], 1.0)
         cos_feat = const.tile([P, 4, P], F32, name="cos_feat")
         sin_feat = const.tile([P, 4, P], F32, name="sin_feat")
 
@@ -287,12 +284,15 @@ def tile_dualmultiheadattention_pa_kernel(
             )
             by_sin = products_pool.tile([P, tiles, P], F32, name="by_sin")
             nc.vector.tensor_tensor(
-                out=by_sin[:].rearrange("p s (j e) -> p s j e", e=2),
-                in0=bank[:, 0 : P * tiles].rearrange("p (s j e) -> p s j e", s=tiles, e=2)[:, :, :, ::-1],
-                in1=table_of(u, sin_tab).rearrange("p s (j e) -> p s j e", e=2),
-                op=MULT,
+                out=by_sin[:], in0=bank[:, 0 : P * tiles].rearrange("p (s c) -> p s c", c=P),
+                in1=table_of(u, sin_src), op=MULT,
             )
-            nc.gpsimd.tensor_tensor(out=y_of[u], in0=by_cos[:], in1=by_sin[:], op=ADD)
+            nc.gpsimd.tensor_tensor(
+                out=y_of[u].rearrange("p s (j e) -> p s j e", e=2),
+                in0=by_cos[:].rearrange("p s (j e) -> p s j e", e=2),
+                in1=by_sin[:].rearrange("p s (j e) -> p s j e", e=2)[:, :, :, ::-1],
+                op=ADD,
+            )
             store(u)
 
         for g in range(PASSES):

from contextlib import ExitStack

import concourse.masks as masks
import concourse.mybir as mybir

F32 = mybir.dt.float32
BF16 = mybir.dt.bfloat16
U32 = mybir.dt.uint32
U8 = mybir.dt.uint8
FP8X4 = mybir.dt.float8_e4m3fn_x4
MULT = mybir.AluOpType.mult
ADD = mybir.AluOpType.add
IDENTITY = mybir.ActivationFunctionType.Identity

P = 128
D = 1024
PASSES = 2
WIDE = 512
N1 = 384
Q_SCALE = P ** -0.5
FLOPS = 2 * 2048 * 1024 * 2048


def tile_dualmultiheadattention_pa_kernel(
    tc, x_1, x_2, cos1, sin1, cos2, sin2, wq1, bq1, wk1, bk1, wq2, bq2, wk2, bk2, out_0, out_1
):
    nc = tc.nc
    projections = [
        (wq1, bq1, out_0, Q_SCALE, (0, 1, 2, 3)),
        (wk1, bk1, out_1, 1.0, (0, 1, 2, 3)),
        (wq2, bq2, out_0, Q_SCALE, (4,)),
        (wk2, bk2, out_1, 1.0, (4,)),
    ]
    units = [(sl, grp, hh) for sl in range(8) for grp in projections[sl // 2][4] for hh in range(4)]
    n_units = len(units)
    group_tiles = [3, 3, 3, 3, 4]

    with ExitStack() as ctx:
        const = ctx.enter_context(tc.tile_pool(name="const", bufs=1))
        raw = ctx.enter_context(tc.tile_pool(name="raw", bufs=1))
        x_grouped_pool = ctx.enter_context(tc.tile_pool(name="x_grouped", bufs=2))
        w_grouped_pool = ctx.enter_context(tc.tile_pool(name="w_grouped", bufs=2))
        w_codes_pool = ctx.enter_context(tc.tile_pool(name="w_codes", bufs=4))
        biased_pool = ctx.enter_context(tc.tile_pool(name="biased", bufs=3))
        turned_pool = ctx.enter_context(tc.tile_pool(name="turned", bufs=3))
        products_pool = ctx.enter_context(tc.tile_pool(name="products", bufs=3))
        y_pool = ctx.enter_context(tc.tile_pool(name="y", bufs=4))
        mx_banks = ctx.enter_context(tc.psum_pool(name="mx_banks", bufs=3))
        back_banks = ctx.enter_context(tc.psum_pool(name="back_banks", bufs=5))
        ctx.enter_context(tc.manual_schedule())

        ident = const.tile([P, P], F32, name="ident")
        masks.make_identity(nc, ident[:])
        one_column = const.tile([P, 1], F32, name="one_column")
        nc.vector.memset(one_column[:], 0.0)
        table_loaded = const.tile([P, 1], F32, name="table_loaded")
        nc.scalar.activation(out=table_loaded[:], in_=one_column[:], func=IDENTITY, bias=one_column[:], scale=1.0)

        bias_rows = const.tile([P, P], BF16, name="bias_rows")
        nc.vector.memset(bias_rows[:], 0.0)
        w_raw = [raw.tile([P, PASSES, 4, WIDE], BF16, name="w_raw%d" % sl) for sl in range(8)]

        def load_slice(sl):
            rows = projections[sl // 2][0].rearrange("(g q t) c -> g q t c", g=PASSES, t=4)
            first = WIDE * (sl % 2)
            for g in range(PASSES):
                nc.sync.dma_start(out=w_raw[sl][:, g, :, :], in_=rows[g, :, :, first : first + WIDE])

        x_raw = [raw.tile([P, group_tiles[g], D], BF16, name="x_raw%d" % g) for g in range(5)]

        def load_x1(b):
            nc.sync.dma_start(out=x_raw[b][:], in_=x_1[b].rearrange("(p j) k -> p j k", j=3))

        cos_bf = const.tile([P, 4, P], BF16, name="cos_bf")
        sin_bf = const.tile([P, 4, P], BF16, name="sin_bf")
        load_slice(0)
        load_x1(0)
        for w in range(4):
            nc.sync.dma_start(
                out=bias_rows[8 * w : 8 * w + 8, :], in_=projections[w][1].rearrange("(h c) -> h c", c=P)
            )
        nc.sync.dma_start(out=cos_bf[:, 0:3, :], in_=cos1.rearrange("(p j) c -> p j c", j=3))
        nc.sync.dma_start(out=sin_bf[:, 0:3, :], in_=sin1.rearrange("(p j) c -> p j c", j=3))
        nc.sync.dma_start(out=cos_bf[:, 3, :], in_=cos2)
        nc.sync.dma_start(out=sin_bf[:, 3, :], in_=sin2)
        load_x1(1)
        load_x1(2)
        load_slice(1)
        load_x1(3)
        load_slice(2)
        nc.sync.dma_start(out=x_raw[4][:], in_=x_2.rearrange("b p k -> p b k"))
        for sl in range(3, 8):
            load_slice(sl)

        def widen(out, in_, factor):
            nc.gpsimd.tensor_scalar(out=out, in0=in_, scalar1=factor, scalar2=0.0, op0=MULT, op1=ADD)

        bias_f32 = const.tile([P, P], F32, name="bias_f32")
        widen(bias_f32[:], bias_rows[:], 1.0)
        swap = const.tile([P, P], F32, name="swap")
        swap_pairs = swap[:].rearrange("p (j e) -> p j e", e=2)
        ident_pairs = ident[:].rearrange("p (j e) -> p j e", e=2)
        for e in range(2):
            widen(swap_pairs[:, :, e], ident_pairs[:, :, 1 - e], 1.0)
        cos_tab = const.tile([P, 4, P], F32, name="cos_tab")
        widen(cos_tab[:], cos_bf[:], 1.0)
        sin_src = const.tile([P, 4, P], F32, name="sin_src")
        sin_bf_pairs = sin_bf[:].rearrange("p s (j e) -> p s j e", e=2)
        sin_src_pairs = sin_src[:].rearrange("p s (j e) -> p s j e", e=2)
        widen(sin_src_pairs[:, :, :, 1], sin_bf_pairs[:, :, :, 0], -1.0)
        widen(sin_src_pairs[:, :, :, 0], sin_bf_pairs[:, :, :, 1], 1.0)
        cos_feat = const.tile([P, 4, P], F32, name="cos_feat")
        sin_feat = const.tile([P, 4, P], F32, name="sin_feat")

        x_codes = [
            const.tile([P, PASSES, P * group_tiles[g]], U32, name="x_codes%d" % g, align_bytes=64) for g in range(5)
        ]
        x_scales = [
            const.tile([P, PASSES, P * group_tiles[g]], U8, name="x_scales%d" % g, align_bytes=64) for g in range(5)
        ]
        x_grouped = {}

        def transpose_x(grp, tl, copy):
            if tl == 0:
                x_grouped[grp] = x_grouped_pool.tile(
                    [P, PASSES, P * group_tiles[grp], 4], BF16, name="x_grouped", align_bytes=64
                )
            words = x_grouped[grp][:].bitcast(F32)
            tokens = x_raw[grp][:, tl, :].bitcast(F32)
            bank = back_banks.tile([P, WIDE], F32, name="back_bank")
            for m in range(2 * PASSES):
                first = 2 * P * (m // 2) + m % 2
                nc.tensor.transpose(
                    bank[:, P * m : P * m + P], tokens[:, first : 2 * P * (m // 2 + 1) : 2], ident[:]
                )
            copy(
                out=words[:, :, P * tl : P * tl + P, :],
                in_=bank[:].rearrange("p (g u t) -> p g t u", g=PASSES, u=2),
            )

        def quantise(codes, scales, grouped):
            words = codes[:].rearrange("p g c -> p (g c)")
            planes = scales[:].rearrange("p g c -> p (g c)")
            values = grouped[:].rearrange("p g c t -> p (g c t)")
            count = words.shape[1]
            first = 0
            for width in (1024, 512, 256):
                if count - first >= width:
                    nc.vector.quantize_mx(
                        out=words[:, first : first + width].bitcast(FP8X4),
                        scales=planes[:, first : first + width],
                        in_=values[:, 4 * first : 4 * (first + width)],
                    )
                    first += width

        def quantise_x(grp):
            quantise(x_codes[grp], x_scales[grp], x_grouped[grp])

        w_grouped = {}
        w_codes = {}

        def regroup_w(sl, g, first, last, copy):
            if g == 0 and first == 0:
                w_grouped[sl] = w_grouped_pool.tile([P, PASSES, WIDE, 4], BF16, name="w_grouped", align_bytes=64)
            copy(
                out=w_grouped[sl][:, g, first:last, :].rearrange("p (c i) t -> p c t i", i=4),
                in_=w_raw[sl][:, g, :, first:last].rearrange("p t (c i) -> p c t i", i=4),
            )

        def quantise_w(sl):
            codes = w_codes_pool.tile([P, PASSES, WIDE], U32, name="w_code_words", align_bytes=64)
            scales = w_codes_pool.tile([P, PASSES, WIDE], U8, name="w_scales", align_bytes=64)
            quantise(codes, scales, w_grouped[sl])
            w_codes[sl] = (codes, scales)

        bias_cols = const.tile([P, 32], F32, name="bias_cols")
        bias_raw = const.tile([P, 32], F32, name="bias_raw")
        mx_bank_of = {}

        def project(u):
            sl, grp, hh = units[u]
            codes, scales = w_codes[sl]
            bank = mx_banks.tile([P, WIDE], F32, name="mx_bank")
            for first, count in ((0, 256), (256, 128)) if grp < 4 else ((0, 512),):
                for g in range(PASSES):
                    nc.tensor.matmul_mx(
                        out=bank[:, first : first + count],
                        lhsT=codes[:, g, P * hh : P * hh + P].bitcast(FP8X4),
                        lhsT_scale=scales[:, g, P * hh : P * hh + P],
                        rhs=x_codes[grp][:, g, first : first + count].bitcast(FP8X4),
                        rhs_scale=x_scales[grp][:, g, first : first + count],
                        start=(g == 0),
                        stop=(g == PASSES - 1),
                    )
            mx_bank_of[u] = bank

        def table_of(u, table):
            if units[u][1] < 4:
                return table[:, 0:3, :]
            return table[:, 3, :].unsqueeze(1).to_broadcast([P, 4, P])

        def tiles_of(u):
            return group_tiles[units[u][1]]

        biased = {}

        def add_bias(u):
            sl, grp, hh = units[u]
            n = P * tiles_of(u)
            t = biased_pool.tile([P, WIDE], F32, name="biased")
            col = 4 * sl + hh
            nc.scalar.activation(
                out=t[:, 0:n], in_=mx_bank_of[u][:, 0:n], func=IDENTITY, bias=bias_cols[:, col : col + 1],
                scale=projections[sl // 2][3],
            )
            biased[u] = t

        back = {}

        def transpose_back(u):
            bank = back_banks.tile([P, WIDE], F32, name="back_bank")
            for tl in range(tiles_of(u)):
                cols = slice(P * tl, P * tl + P)
                nc.tensor.transpose(bank[:, cols], biased[u][:, cols], ident[:])
            back[u] = bank

        turned = {}

        def turn(u):
            sl, grp, hh = units[u]
            tiles = tiles_of(u)
            col = 4 * sl + hh
            turned[u] = []
            for table, name in ((cos_feat, "turned_cos"), (sin_feat, "turned_sin")):
                t = turned_pool.tile([P, WIDE], F32, name=name)
                nc.vector.scalar_tensor_tensor(
                    out=t[:, 0 : P * tiles].rearrange("p (s t) -> p s t", t=P),
                    in0=mx_bank_of[u][:, 0 : P * tiles].rearrange("p (s t) -> p s t", t=P),
                    scalar=bias_raw[:, col : col + 1], in1=table_of(u, table), op0=ADD, op1=MULT,
                )
                turned[u].append(t)

        def merge_back(u):
            bank = back_banks.tile([P, WIDE], F32, name="back_bank")
            for tl in range(tiles_of(u)):
                cols = slice(P * tl, P * tl + P)
                by_cos, by_sin = turned[u]
                nc.tensor.matmul(bank[:, cols], lhsT=by_cos[:, cols], rhs=ident[:], is_transpose=True, start=True, stop=False)
                nc.tensor.matmul(bank[:, cols], lhsT=by_sin[:, cols], rhs=swap[:], is_transpose=True, start=False, stop=True)
            back[u] = bank

        y_of = {}

        def open_y(u):
            y = y_pool.tile([P, 2, tiles_of(u), P], F32, name="y")
            y_of[u] = y[:, 0, :, :]
            y_of[u + 1] = y[:, 1, :, :]

        def store(u):
            sl, grp, hh = units[u]
            heads = projections[sl // 2][2]
            h = 4 * (sl % 2) + hh
            if grp < 4:
                nc.sync.dma_start(
                    out=heads[grp, h, 0:N1, :].rearrange("(p j) c -> p j c", j=3), in_=y_of[u]
                )
            else:
                nc.sync.dma_start(out=heads[:, h, N1:WIDE, :].rearrange("b p c -> p b c"), in_=y_of[u])

        def leave_merged(u):
            nc.scalar.mul(
                out=y_of[u], in_=back[u][:, 0 : P * tiles_of(u)].rearrange("p (s c) -> p s c", c=P),
                mul=projections[units[u][0] // 2][3],
            )
            store(u)

        def rope(u):
            tiles = tiles_of(u)
            bank = back[u]
            by_cos = products_pool.tile([P, tiles, P], F32, name="by_cos")
            nc.vector.tensor_tensor(
                out=by_cos[:], in0=bank[:, 0 : P * tiles].rearrange("p (s c) -> p s c", c=P),
                in1=table_of(u, cos_tab), op=MULT,
            )
            by_sin = products_pool.tile([P, tiles, P], F32, name="by_sin")
            nc.vector.tensor_tensor(
                out=by_sin[:], in0=bank[:, 0 : P * tiles].rearrange("p (s c) -> p s c", c=P),
                in1=table_of(u, sin_src), op=MULT,
            )
            nc.gpsimd.tensor_tensor(
                out=y_of[u].rearrange("p s (j e) -> p s j e", e=2),
                in0=by_cos[:].rearrange("p s (j e) -> p s j e", e=2),
                in1=by_sin[:].rearrange("p s (j e) -> p s j e", e=2)[:, :, :, ::-1],
                op=ADD,
            )
            store(u)

        for g in range(PASSES):
            regroup_w(0, g, 0, WIDE, nc.vector.tensor_copy)
        quantise_w(0)
        for tl in range(3):
            transpose_x(0, tl, nc.scalar.copy)
        quantise_x(0)
        bias_bank = back_banks.tile([P, WIDE], F32, name="back_bank")
        nc.tensor.transpose(bias_bank[:, 0:P], bias_f32[:], ident[:])
        nc.scalar.copy(out=bias_raw[:], in_=bias_bank[:, 0:32])
        for w in range(4):
            nc.scalar.mul(out=bias_cols[:, 8 * w : 8 * w + 8], in_=bias_raw[:, 8 * w : 8 * w + 8], mul=projections[w][3])
        project(0)
        project(1)
        add_bias(0)
        for tab, feat in ((cos_tab, cos_feat), (sin_src, sin_feat)):
            feat_bank = back_banks.tile([P, WIDE], F32, name="back_bank")
            for slot in range(4):
                nc.tensor.transpose(feat_bank[:, P * slot : P * slot + P], tab[:, slot, :], ident[:])
            nc.scalar.copy(out=feat[:].rearrange("p s t -> p (s t)"), in_=feat_bank[:])
        turn(1)

        x_group_of_step = {0: (1, 0, 3), 1: (2, 0, 3), 3: (3, 0, 3), 10: (4, 0, 2), 11: (4, 2, 4)}
        pieces = [(sl, g, c) for sl in range(1, 8) for g in range(PASSES) for c in range(4)]
        for i in range(n_units // 2):
            u = 2 * i
            if u + 2 < n_units:
                project(u + 2)
                project(u + 3)
                add_bias(u + 2)
            open_y(u)
            transpose_back(u)
            merge_back(u + 1)
            if i in x_group_of_step:
                grp, tl0, tl1 = x_group_of_step[i]
                for tl in range(tl0, tl1):
                    transpose_x(grp, tl, nc.scalar.copy)
            mine = pieces[7 * (i - 1) // 4 : 7 * i // 4] if i > 0 else []
            for sl, g, c in mine:
                regroup_w(sl, g, P * c, P * c + P, nc.scalar.copy)
            leave_merged(u + 1)
            if u + 2 < n_units:
                turn(u + 3)
            rope(u)
            if i in x_group_of_step and tl1 == group_tiles[grp]:
                quantise_x(grp)
            for sl, g, c in mine:
                if (g, c) == (PASSES - 1, 3):
                    quantise_w(sl)
